import numpy as np
import ml_dtypes


def mxq(x, axis, fmt="e4m3"):
    dtype, down = {"e4m3": (ml_dtypes.float8_e4m3fn, 7), "e5m2": (ml_dtypes.float8_e5m2, 14)}[fmt]
    v = np.moveaxis(np.asarray(x, np.float32).astype(ml_dtypes.bfloat16).astype(np.float64), axis, -1)
    blocks = v.reshape(v.shape[:-1] + (-1, 32))
    amax = np.abs(blocks).max(-1, keepdims=True)
    byte = np.maximum(np.where(amax > 0, np.frexp(amax)[1] - 1 + 127, 0) - down, 1)
    scale = np.exp2(byte - 127.0)
    codes = (blocks / scale).astype(np.float32).astype(dtype).astype(np.float64)
    return np.moveaxis((codes * scale).reshape(v.shape), -1, axis)


WIDE = False


def mx_kscale(k):
    if not WIDE:
        return np.ones(k)
    levels = np.array([10, -10, 5, -5, 0])
    a = np.random.permutation(np.resize(levels, k // 512 * 4)).reshape(k // 512, 4)
    idx = np.arange(k)
    return np.exp2(a[idx // 512, idx % 128 // 32])


BF16 = ml_dtypes.bfloat16


def bf(x):
    return np.asarray(x, np.float32).astype(BF16)


def f64(x):
    return np.asarray(x).astype(np.float64)


E2M1 = np.array([0.0, 0.5, 1.0, 1.5, 2.0, 3.0, 4.0, 6.0, -0.0, -0.5, -1.0, -1.5, -2.0, -3.0, -4.0, -6.0])


def pack_weight(w, fmt):
    k, n = w.shape
    w = f64(bf(w)).reshape(k // 32, 32, n)
    amax = np.abs(w).max(1)
    if fmt == "e4m3":
        byte = np.frexp(amax)[1] - 1 + 127 - 7
    else:
        mant, ex = np.frexp(amax / 6.0)
        byte = np.where(mant > 0.5, ex, ex - 1) + 127
    byte = np.clip(np.where(amax > 0, byte, 1), 1, 254)
    scaled = (w * np.exp2(127.0 - byte)[:, None, :]).reshape(k, n).astype(np.float32)
    by_word = np.ascontiguousarray(scaled.reshape(k // 512, 128, 4, n).transpose(0, 1, 3, 2))
    if fmt == "e4m3":
        words = by_word.astype(ml_dtypes.float8_e4m3fn).view(np.uint8)
    else:
        c = by_word.astype(ml_dtypes.float4_e2m1fn).view(np.uint8) & 0xF
        words = c[..., 0::2] | (c[..., 1::2] << 4)
    return np.ascontiguousarray(words), np.ascontiguousarray(byte.astype(np.uint8).reshape(k // 512, 16, n))


def unpack_weight(words, scales, fmt):
    g, p, n, _ = words.shape
    if fmt == "e4m3":
        vals = np.ascontiguousarray(words).view(ml_dtypes.float8_e4m3fn).astype(np.float64)
    else:
        nib = np.empty((g, p, n, 4), np.uint8)
        nib[..., 0::2] = words & 0xF
        nib[..., 1::2] = words >> 4
        vals = E2M1[nib]
    vals = vals * np.repeat(np.exp2(scales.astype(np.float64) - 127.0), 8, axis=1)[..., None]
    return vals.transpose(0, 1, 3, 2).reshape(g * 512, n)


B, T, D, H, DH, F = 4, 256, 1024, 16, 64, 4096
A = H * DH
EPS = 1e-6
FMT = "e4m3"


def layer_norm(v, gain, bias):
    mu = v.mean(-1, keepdims=True)
    var = np.square(v - mu).mean(-1, keepdims=True)
    return (v - mu) * (1.0 / np.sqrt(var + EPS)) * gain + bias


def setup_inputs():
    s = mx_kscale(D)
    r = np.random.standard_normal
    x = bf(r((B, T, D)))
    ln1_gain = bf((1.0 + 0.1 * r(D)) * s)
    ln1_bias = bf(0.1 * r(D) * s)
    wq_words, wq_scales = pack_weight(r((D, A)) / np.sqrt(D) / s[:, None], FMT)
    bq = bf(0.1 * r(A))
    wk_words, wk_scales = pack_weight(r((D, A)) / np.sqrt(D) / s[:, None], FMT)
    bk = bf(0.1 * r(A))
    wv_words, wv_scales = pack_weight(r((D, A)) / np.sqrt(D) / s[:, None], FMT)
    bv = bf(0.1 * r(A))
    return {"x": x,
            "ln1_gain": ln1_gain,
            "ln1_bias": ln1_bias,
            "wq_words": wq_words,
            "wq_scales": wq_scales,
            "bq": bq,
            "wk_words": wk_words,
            "wk_scales": wk_scales,
            "bk": bk,
            "wv_words": wv_words,
            "wv_scales": wv_scales,
            "bv": bv}


def reference(x, ln1_gain, ln1_bias, wq_words, wq_scales, bq, wk_words, wk_scales, bk, wv_words, wv_scales, bv):
    h = layer_norm(f64(x), f64(ln1_gain), f64(ln1_bias))
    hq = mxq(h, 2, "e4m3")
    q = ((hq @ unpack_weight(wq_words, wq_scales, FMT)) + f64(bq)).reshape(B, T, H, DH)
    k = ((hq @ unpack_weight(wk_words, wk_scales, FMT)) + f64(bk)).reshape(B, T, H, DH)
    v = ((hq @ unpack_weight(wv_words, wv_scales, FMT)) + f64(bv)).reshape(B, T, H, DH)
    return q, k, v

@@ -1,0 +1,267 @@
+from contextlib import ExitStack
+
+import concourse.mybir as mybir
+from concourse.masks import make_identity
+
+F32 = mybir.dt.float32
+BF16 = mybir.dt.bfloat16
+I32 = mybir.dt.int32
+U32 = mybir.dt.uint32
+U8 = mybir.dt.uint8
+FP8X4 = mybir.dt.float8_e4m3fn_x4
+ALU = mybir.AluOpType
+ACT = mybir.ActivationFunctionType
+
+P = 128
+PACK = 4
+K_PASS = P * PACK
+TOKENS = 4 * 256
+D = 1024
+A = 1024
+EPS = 1e-6
+N_TILES = TOKENS // P
+PASSES = D // K_PASS
+CHUNK = 512
+CHUNKS = A // CHUNK
+WEIGHTS = 3
+QUADRANTS = 4
+SCALE_ROWS = 4
+
+LEAD_STATS = 4
+LEAD_NORMALISE = 3
+LEAD_TRANSPOSE = 2
+LEAD_QUANTISE = 1
+
+FLOPS = 2 * TOKENS * D * WEIGHTS * A
+
+
+def tile_swidtblock_pa_kernel(
+    tc,
+    x,
+    ln1_gain,
+    ln1_bias,
+    wq_words,
+    wq_scales,
+    bq,
+    wk_words,
+    wk_scales,
+    bk,
+    wv_words,
+    wv_scales,
+    bv,
+    out_0,
+    out_1,
+    out_2,
+):
+    nc = tc.nc
+    x_rows = x.rearrange("b t d -> (b t) d")
+    words_in = [wq_words, wk_words, wv_words]
+    scales_in = [wq_scales, wk_scales, wv_scales]
+    biases_in = [bq, bk, bv]
+    outs = [o.rearrange("b t h d -> (b t) (h d)") for o in (out_0, out_1, out_2)]
+
+    with ExitStack() as ctx:
+        ctx.enter_context(tc.manual_schedule())
+        keep = ctx.enter_context(tc.tile_pool(name="keep", bufs=1))
+        small = ctx.enter_context(tc.tile_pool(name="small", bufs=6))
+        work = ctx.enter_context(tc.tile_pool(name="work", bufs=3))
+        results = ctx.enter_context(tc.tile_pool(name="results", bufs=8))
+        banks = ctx.enter_context(tc.psum_pool(name="banks", bufs=6))
+        flipped = ctx.enter_context(tc.psum_pool(name="flipped", bufs=2))
+
+        x_tiles = []
+        for i in range(N_TILES):
+            x_tile = keep.tile([P, D], BF16, name="x%d" % i)
+            x_tiles.append(x_tile)
+        w_words = []
+        for w in range(WEIGHTS):
+            w_tile = keep.tile([P, PASSES, A], U32, name="w_words%d" % w, align_bytes=64)
+            w_words.append(w_tile)
+        w_planes = keep.tile([P, WEIGHTS * A], U8, align_bytes=64)
+        bias_rows = keep.tile([P, WEIGHTS * A], BF16)
+        bias_all = keep.tile([P, WEIGHTS * A], F32)
+        ones = keep.tile([P, P], BF16)
+        ident = keep.tile([P, P], F32)
+        minus_half = keep.tile([P, 1], F32)
+        gain_bf = keep.tile([P, PASSES, PACK], BF16)
+        beta_bf = keep.tile([P, PASSES, PACK], BF16)
+        gain_col = keep.tile([P, PASSES * PACK], F32)
+        beta_col = keep.tile([P, PASSES * PACK], F32)
+
+        nc.vector.memset(w_planes[:].bitcast(I32), 0)
+        nc.vector.memset(bias_rows[:], 0.0)
+        nc.vector.memset(ones[:], 1.0)
+        nc.gpsimd.memset(minus_half[:], -0.5)
+        make_identity(nc, ident[:])
+
+        def load_x(i):
+            nc.sync.dma_start(out=x_tiles[i][:], in_=x_rows[i * P : (i + 1) * P, :])
+
+        def load_scales(w):
+            for quadrant in range(QUADRANTS):
+                first = 32 * quadrant
+                rows = slice(SCALE_ROWS * quadrant, SCALE_ROWS * (quadrant + 1))
+                nc.sync.dma_start(
+                    out=w_planes[first : first + PASSES * SCALE_ROWS, w * A : (w + 1) * A].bitcast(I32),
+                    in_=scales_in[w][:, rows, :].bitcast(I32),
+                )
+
+        def load_words(w):
+            for g in range(PASSES):
+                nc.sync.dma_start(
+                    out=w_words[w][:, g, :].bitcast(I32),
+                    in_=words_in[w][g].rearrange("p n t -> p (n t)").bitcast(I32),
+                )
+
+        load_x(0)
+        for w in range(WEIGHTS):
+            load_scales(w)
+        load_x(1)
+        load_x(2)
+        load_words(0)
+        load_x(3)
+        load_words(1)
+        load_words(2)
+        for i in range(4, N_TILES):
+            load_x(i)
+
+        nc.scalar.dma_start(out=gain_bf[:], in_=ln1_gain.rearrange("(g p t) -> p g t", p=P, t=PACK))
+        nc.scalar.dma_start(out=beta_bf[:], in_=ln1_bias.rearrange("(g p t) -> p g t", p=P, t=PACK))
+        for w in range(WEIGHTS):
+            nc.scalar.dma_start(
+                out=bias_rows[0:1, w * A : (w + 1) * A],
+                in_=biases_in[w].rearrange("(o n) -> o n", o=1),
+            )
+
+        for c in range(WEIGHTS * CHUNKS):
+            cols = slice(c * CHUNK, (c + 1) * CHUNK)
+            spread = banks.tile([P, CHUNK], F32, tag="bank")
+            nc.tensor.matmul(out=spread[:], lhsT=ones[:], rhs=bias_rows[:, cols], start=True, stop=True)
+            nc.scalar.copy(out=bias_all[:, cols], in_=spread[:])
+
+        centre = {}
+        n_sorted = {}
+        h_planes = {}
+        h_grouped = {}
+        h_codes = {}
+        h_scales = {}
+
+        def stats(i):
+            partial = small.tile([P, PASSES, 6], F32)
+            for g in range(PASSES):
+                nc.vector.bn_stats(out=partial[:, g, :], in_=x_tiles[i][:, g * K_PASS : (g + 1) * K_PASS])
+            mean_var = small.tile([P, 2], F32)
+            nc.vector.bn_aggr(out=mean_var[:], in_=partial[:].rearrange("p g s -> p (g s)"))
+            shifted = small.tile([P, 2], F32)
+            nc.vector.tensor_scalar(
+                out=shifted[:, 0:1], in0=mean_var[:, 0:1], scalar1=-1.0, scalar2=None, op0=ALU.mult
+            )
+            nc.vector.tensor_scalar(
+                out=shifted[:, 1:2], in0=mean_var[:, 1:2], scalar1=EPS, scalar2=None, op0=ALU.add
+            )
+            centre[i] = shifted
+
+        def normalise(i):
+            shifted = centre[i]
+            rstd = small.tile([P, 1], F32)
+            nc.gpsimd.tensor_tensor(out=rstd[:], in0=shifted[:, 1:2], in1=minus_half[:], op=ALU.pow)
+            for g in range(PASSES):
+                n_half = work.tile([P, K_PASS], F32, bufs=6)
+                nc.gpsimd.tensor_scalar(
+                    out=n_half[:].rearrange("r (t p) -> r t p", t=PACK),
+                    in0=x_tiles[i][:, g * K_PASS : (g + 1) * K_PASS].rearrange("r (p t) -> r t p", t=PACK),
+                    scalar1=shifted[:, 0:1],
+                    scalar2=rstd[:, 0:1],
+                    op0=ALU.add,
+                    op1=ALU.mult,
+                )
+                n_sorted[(i, g)] = n_half
+
+        def transpose_and_scale(i):
+            planes = work.tile([P, PASSES, PACK, P], BF16)
+            for g in range(PASSES):
+                n_half = n_sorted[(i, g)]
+                turned = flipped.tile([P, PACK, P], F32)
+                for t in range(PACK):
+                    nc.tensor.transpose(turned[:, t, :], n_half[:, t * P : (t + 1) * P], ident[:])
+                for t in range(PACK):
+                    col = g * PACK + t
+                    nc.scalar.activation(
+                        out=planes[:, g, t, :],
+                        in_=turned[:, t, :],
+                        func=ACT.Identity,
+                        scale=gain_col[:, col : col + 1],
+                        bias=beta_col[:, col : col + 1],
+                    )
+            h_planes[i] = planes
+
+        def regroup(i):
+            planes = h_planes[i]
+            grouped = work.tile([P, PASSES * P * PACK], BF16, align_bytes=64)
+            nc.scalar.copy(
+                out=grouped[:].rearrange("p (g r t) -> p g r t", g=PASSES, t=PACK),
+                in_=planes[:].rearrange("p g t r -> p g r t"),
+            )
+            h_grouped[i] = grouped
+
+        def quantise(i):
+            grouped = h_grouped[i]
+            codes = work.tile([P, PASSES * P], U32, align_bytes=64)
+            scales = work.tile([P, PASSES * P], U8, align_bytes=64)
+            nc.vector.quantize_mx(out=codes[:].bitcast(FP8X4), scales=scales[:], in_=grouped[:])
+            h_codes[i] = codes
+            h_scales[i] = scales
+
+        def project(i):
+            codes = h_codes[i]
+            scales = h_scales[i]
+            token_rows = slice(i * P, (i + 1) * P)
+            finished = []
+            for w in range(WEIGHTS):
+                result = results.tile([P, A], F32)
+                for c in range(CHUNKS):
+                    cols = slice(c * CHUNK, (c + 1) * CHUNK)
+                    bias_cols = slice(w * A + c * CHUNK, w * A + (c + 1) * CHUNK)
+                    acc = banks.tile([P, CHUNK], F32, tag="bank")
+                    for g in range(PASSES):
+                        tokens = slice(g * P, (g + 1) * P)
+                        nc.tensor.matmul_mx(
+                            out=acc[:],
+                            lhsT=codes[:, tokens].bitcast(FP8X4),
+                            lhsT_scale=scales[:, tokens],
+                            rhs=w_words[w][:, g, cols].bitcast(FP8X4),
+                            rhs_scale=w_planes[SCALE_ROWS * g : P, bias_cols],
+                            start=(g == 0),
+                            stop=(g == PASSES - 1),
+                        )
+                    if w == 0:
+                        nc.scalar.copy(out=result[:, cols], in_=acc[:])
+                        nc.gpsimd.tensor_tensor(
+                            out=result[:, cols], in0=result[:, cols], in1=bias_all[:, bias_cols], op=ALU.add
+                        )
+                    else:
+                        nc.vector.tensor_tensor(
+                            out=result[:, cols], in0=acc[:], in1=bias_all[:, bias_cols], op=ALU.add
+                        )
+                finished.append(result)
+            for w in (1, 2, 0):
+                nc.sync.dma_start(out=outs[w][token_rows, :], in_=finished[w][:])
+
+        def in_range(i):
+            return 0 <= i < N_TILES
+
+        for s in range(-LEAD_STATS, N_TILES):
+            if in_range(s + LEAD_QUANTISE):
+                quantise(s + LEAD_QUANTISE)
+            if in_range(s):
+                project(s)
+            if in_range(s + LEAD_TRANSPOSE):
+                transpose_and_scale(s + LEAD_TRANSPOSE)
+                regroup(s + LEAD_TRANSPOSE)
+            if in_range(s + LEAD_STATS):
+                stats(s + LEAD_STATS)
+            if s == -LEAD_STATS:
+                nc.vector.tensor_copy(out=gain_col[:], in_=gain_bf[:].rearrange("p g t -> p (g t)"))
+                nc.vector.tensor_copy(out=beta_col[:], in_=beta_bf[:].rearrange("p g t -> p (g t)"))
+            if in_range(s + LEAD_NORMALISE):
+                normalise(s + LEAD_NORMALISE)

@@ -32,6 +32,9 @@ LEAD_NORMALISE = 3
 LEAD_TRANSPOSE = 2
 LEAD_QUANTISE = 1
 
+SINGLE_X_LOADS = 4
+LONG_WAY = 0
+
 FLOPS = 2 * TOKENS * D * WEIGHTS * A
 
 
@@ -65,21 +68,27 @@ def tile_swidtblock_pa_kernel(
         keep = ctx.enter_context(tc.tile_pool(name="keep", bufs=1))
         small = ctx.enter_context(tc.tile_pool(name="small", bufs=6))
         work = ctx.enter_context(tc.tile_pool(name="work", bufs=3))
-        results = ctx.enter_context(tc.tile_pool(name="results", bufs=8))
+        results = ctx.enter_context(tc.tile_pool(name="results", bufs=16))
         banks = ctx.enter_context(tc.psum_pool(name="banks", bufs=6))
         flipped = ctx.enter_context(tc.psum_pool(name="flipped", bufs=2))
 
         x_tiles = []
-        for i in range(N_TILES):
+        for i in range(SINGLE_X_LOADS):
             x_tile = keep.tile([P, D], BF16, name="x%d" % i)
-            x_tiles.append(x_tile)
+            x_tiles.append(x_tile[:])
+        x_rest = keep.tile([P, N_TILES - SINGLE_X_LOADS, D], BF16)
+        for i in range(SINGLE_X_LOADS, N_TILES):
+            x_tiles.append(x_rest[:, i - SINGLE_X_LOADS, :])
         w_words = []
         for w in range(WEIGHTS):
             w_tile = keep.tile([P, PASSES, A], U32, name="w_words%d" % w, align_bytes=64)
             w_words.append(w_tile)
-        w_planes = keep.tile([P, WEIGHTS * A], U8, align_bytes=64)
+        w_planes = []
+        for w in range(WEIGHTS):
+            plane_tile = keep.tile([P, A], U8, name="w_planes%d" % w, align_bytes=64)
+            w_planes.append(plane_tile)
         bias_rows = keep.tile([P, WEIGHTS * A], BF16)
-        bias_all = keep.tile([P, WEIGHTS * A], F32)
+        bias_all = keep.tile([P, WEIGHTS * A], BF16)
         ones = keep.tile([P, P], BF16)
         ident = keep.tile([P, P], F32)
         minus_half = keep.tile([P, 1], F32)
@@ -88,56 +97,65 @@ def tile_swidtblock_pa_kernel(
         gain_col = keep.tile([P, PASSES * PACK], F32)
         beta_col = keep.tile([P, PASSES * PACK], F32)
 
-        nc.vector.memset(w_planes[:].bitcast(I32), 0)
         nc.vector.memset(bias_rows[:], 0.0)
+        for w in range(WEIGHTS):
+            nc.vector.memset(w_planes[w][:].bitcast(I32), 0)
         nc.vector.memset(ones[:], 1.0)
         nc.gpsimd.memset(minus_half[:], -0.5)
         make_identity(nc, ident[:])
 
         def load_x(i):
-            nc.sync.dma_start(out=x_tiles[i][:], in_=x_rows[i * P : (i + 1) * P, :])
+            nc.sync.dma_start(out=x_tiles[i], in_=x_rows[i * P : (i + 1) * P, :])
 
         def load_scales(w):
             for quadrant in range(QUADRANTS):
                 first = 32 * quadrant
                 rows = slice(SCALE_ROWS * quadrant, SCALE_ROWS * (quadrant + 1))
                 nc.sync.dma_start(
-                    out=w_planes[first : first + PASSES * SCALE_ROWS, w * A : (w + 1) * A].bitcast(I32),
+                    out=w_planes[w][first : first + PASSES * SCALE_ROWS, :].bitcast(I32),
                     in_=scales_in[w][:, rows, :].bitcast(I32),
                 )
 
         def load_words(w):
-            for g in range(PASSES):
-                nc.sync.dma_start(
-                    out=w_words[w][:, g, :].bitcast(I32),
-                    in_=words_in[w][g].rearrange("p n t -> p (n t)").bitcast(I32),
-                )
+            nc.sync.dma_start(
+                out=w_words[w][:].bitcast(I32),
+                in_=words_in[w].rearrange("g p n t -> p g (n t)").bitcast(I32),
+            )
 
         load_x(0)
-        for w in range(WEIGHTS):
-            load_scales(w)
-        load_x(1)
-        load_x(2)
-        load_words(0)
-        load_x(3)
-        load_words(1)
-        load_words(2)
-        for i in range(4, N_TILES):
-            load_x(i)
-
-        nc.scalar.dma_start(out=gain_bf[:], in_=ln1_gain.rearrange("(g p t) -> p g t", p=P, t=PACK))
-        nc.scalar.dma_start(out=beta_bf[:], in_=ln1_bias.rearrange("(g p t) -> p g t", p=P, t=PACK))
         for w in range(WEIGHTS):
             nc.scalar.dma_start(
                 out=bias_rows[0:1, w * A : (w + 1) * A],
                 in_=biases_in[w].rearrange("(o n) -> o n", o=1),
             )
+        load_x(1)
+        load_words(0)
+        nc.scalar.dma_start(out=gain_bf[:], in_=ln1_gain.rearrange("(g p t) -> p g t", p=P, t=PACK))
+        nc.scalar.dma_start(out=beta_bf[:], in_=ln1_bias.rearrange("(g p t) -> p g t", p=P, t=PACK))
+        load_scales(0)
+        load_x(2)
+        load_words(1)
+        load_scales(1)
+        load_words(2)
+        load_scales(2)
+        load_x(3)
+        nc.sync.dma_start(
+            out=x_rest[:],
+            in_=x_rows[SINGLE_X_LOADS * P :, :].rearrange("(i p) d -> p i d", p=P),
+        )
 
-        for c in range(WEIGHTS * CHUNKS):
-            cols = slice(c * CHUNK, (c + 1) * CHUNK)
-            spread = banks.tile([P, CHUNK], F32, tag="bank")
-            nc.tensor.matmul(out=spread[:], lhsT=ones[:], rhs=bias_rows[:, cols], start=True, stop=True)
-            nc.scalar.copy(out=bias_all[:, cols], in_=spread[:])
+        for w in range(WEIGHTS):
+            spread = banks.tile([P, A], BF16, tag="bank")
+            for c in range(CHUNKS):
+                cols = slice(c * CHUNK, (c + 1) * CHUNK)
+                nc.tensor.matmul(
+                    out=spread[:, cols],
+                    lhsT=ones[:],
+                    rhs=bias_rows[:, w * A + c * CHUNK : w * A + (c + 1) * CHUNK],
+                    start=True,
+                    stop=True,
+                )
+            nc.scalar.copy(out=bias_all[:, w * A : (w + 1) * A], in_=spread[:])
 
         centre = {}
         n_sorted = {}
@@ -212,49 +230,49 @@ def tile_swidtblock_pa_kernel(
             h_codes[i] = codes
             h_scales[i] = scales
 
-        def project(i):
-            codes = h_codes[i]
-            scales = h_scales[i]
-            token_rows = slice(i * P, (i + 1) * P)
+        def store(i, w, c, result):
+            nc.sync.dma_start(out=outs[w][i * P : (i + 1) * P, c * CHUNK : (c + 1) * CHUNK], in_=result[:])
+
+        def project(i, w):
             finished = []
-            for w in range(WEIGHTS):
-                result = results.tile([P, A], F32)
-                for c in range(CHUNKS):
-                    cols = slice(c * CHUNK, (c + 1) * CHUNK)
-                    bias_cols = slice(w * A + c * CHUNK, w * A + (c + 1) * CHUNK)
-                    acc = banks.tile([P, CHUNK], F32, tag="bank")
-                    for g in range(PASSES):
-                        tokens = slice(g * P, (g + 1) * P)
-                        nc.tensor.matmul_mx(
-                            out=acc[:],
-                            lhsT=codes[:, tokens].bitcast(FP8X4),
-                            lhsT_scale=scales[:, tokens],
-                            rhs=w_words[w][:, g, cols].bitcast(FP8X4),
-                            rhs_scale=w_planes[SCALE_ROWS * g : P, bias_cols],
-                            start=(g == 0),
-                            stop=(g == PASSES - 1),
-                        )
-                    if w == 0:
-                        nc.scalar.copy(out=result[:, cols], in_=acc[:])
-                        nc.gpsimd.tensor_tensor(
-                            out=result[:, cols], in0=result[:, cols], in1=bias_all[:, bias_cols], op=ALU.add
-                        )
-                    else:
-                        nc.vector.tensor_tensor(
-                            out=result[:, cols], in0=acc[:], in1=bias_all[:, bias_cols], op=ALU.add
-                        )
+            for c in range(CHUNKS):
+                cols = slice(c * CHUNK, (c + 1) * CHUNK)
+                bias_cols = slice(w * A + c * CHUNK, w * A + (c + 1) * CHUNK)
+                result = results.tile([P, CHUNK], F32)
+                acc = banks.tile([P, CHUNK], F32, tag="bank")
+                for g in range(PASSES):
+                    tokens = slice(g * P, (g + 1) * P)
+                    nc.tensor.matmul_mx(
+                        out=acc[:],
+                        lhsT=h_codes[i][:, tokens].bitcast(FP8X4),
+                        lhsT_scale=h_scales[i][:, tokens],
+                        rhs=w_words[w][:, g, cols].bitcast(FP8X4),
+                        rhs_scale=w_planes[w][SCALE_ROWS * g : P, cols],
+                        start=(g == 0),
+                        stop=(g == PASSES - 1),
+                    )
+                if w == LONG_WAY:
+                    nc.scalar.copy(out=result[:], in_=acc[:])
+                    nc.gpsimd.tensor_tensor(out=result[:], in0=result[:], in1=bias_all[:, bias_cols], op=ALU.add)
+                else:
+                    nc.vector.tensor_tensor(out=result[:], in0=acc[:], in1=bias_all[:, bias_cols], op=ALU.add)
+                    store(i, w, c, result)
                 finished.append(result)
-            for w in (1, 2, 0):
-                nc.sync.dma_start(out=outs[w][token_rows, :], in_=finished[w][:])
+            return finished
 
         def in_range(i):
             return 0 <= i < N_TILES
 
         for s in range(-LEAD_STATS, N_TILES):
+            if in_range(s):
+                long_way_results = project(s, 0)
+                project(s, 1)
             if in_range(s + LEAD_QUANTISE):
                 quantise(s + LEAD_QUANTISE)
             if in_range(s):
-                project(s)
+                project(s, 2)
+                for c in range(CHUNKS):
+                    store(s, LONG_WAY, c, long_way_results[c])
             if in_range(s + LEAD_TRANSPOSE):
                 transpose_and_scale(s + LEAD_TRANSPOSE)
                 regroup(s + LEAD_TRANSPOSE)

@@ -89,6 +89,7 @@ def tile_swidtblock_pa_kernel(
             w_planes.append(plane_tile)
         bias_rows = keep.tile([P, WEIGHTS * A], BF16)
         bias_all = keep.tile([P, WEIGHTS * A], BF16)
+        bias_long_way = keep.tile([P, A], F32)
         ones = keep.tile([P, P], BF16)
         ident = keep.tile([P, P], F32)
         minus_half = keep.tile([P, 1], F32)
@@ -97,12 +98,10 @@ def tile_swidtblock_pa_kernel(
         gain_col = keep.tile([P, PASSES * PACK], F32)
         beta_col = keep.tile([P, PASSES * PACK], F32)
 
-        nc.vector.memset(bias_rows[:], 0.0)
+        nc.vector.memset(bias_rows[:].bitcast(I32), 0)
         for w in range(WEIGHTS):
             nc.vector.memset(w_planes[w][:].bitcast(I32), 0)
         nc.vector.memset(ones[:], 1.0)
-        nc.gpsimd.memset(minus_half[:], -0.5)
-        make_identity(nc, ident[:])
 
         def load_x(i):
             nc.sync.dma_start(out=x_tiles[i], in_=x_rows[i * P : (i + 1) * P, :])
@@ -117,27 +116,27 @@ def tile_swidtblock_pa_kernel(
                 )
 
         def load_words(w):
-            nc.sync.dma_start(
-                out=w_words[w][:].bitcast(I32),
-                in_=words_in[w].rearrange("g p n t -> p g (n t)").bitcast(I32),
+            nc.gpsimd.dma_start(
+                out=w_words[w][:].bitcast(F32),
+                in_=words_in[w].rearrange("g p n t -> p g (n t)").bitcast(F32),
             )
 
         load_x(0)
+        nc.gpsimd.memset(minus_half[:], -0.5)
+        make_identity(nc, ident[:])
+        for w in range(WEIGHTS):
+            load_words(w)
         for w in range(WEIGHTS):
             nc.scalar.dma_start(
                 out=bias_rows[0:1, w * A : (w + 1) * A],
                 in_=biases_in[w].rearrange("(o n) -> o n", o=1),
             )
         load_x(1)
-        load_words(0)
+        load_x(2)
         nc.scalar.dma_start(out=gain_bf[:], in_=ln1_gain.rearrange("(g p t) -> p g t", p=P, t=PACK))
         nc.scalar.dma_start(out=beta_bf[:], in_=ln1_bias.rearrange("(g p t) -> p g t", p=P, t=PACK))
-        load_scales(0)
-        load_x(2)
-        load_words(1)
-        load_scales(1)
-        load_words(2)
-        load_scales(2)
+        for w in range(WEIGHTS):
+            load_scales(w)
         load_x(3)
         nc.sync.dma_start(
             out=x_rest[:],
@@ -233,8 +232,10 @@ def tile_swidtblock_pa_kernel(
         def store(i, w, c, result):
             nc.sync.dma_start(out=outs[w][i * P : (i + 1) * P, c * CHUNK : (c + 1) * CHUNK], in_=result[:])
 
-        def project(i, w):
-            finished = []
+        def vector_has_stats(i):
+            return i + LEAD_STATS < N_TILES
+
+        def project(i, w, late_stores):
             for c in range(CHUNKS):
                 cols = slice(c * CHUNK, (c + 1) * CHUNK)
                 bias_cols = slice(w * A + c * CHUNK, w * A + (c + 1) * CHUNK)
@@ -251,28 +252,28 @@ def tile_swidtblock_pa_kernel(
                         start=(g == 0),
                         stop=(g == PASSES - 1),
                     )
-                if w == LONG_WAY:
+                if w == LONG_WAY and vector_has_stats(i):
                     nc.scalar.copy(out=result[:], in_=acc[:])
-                    nc.gpsimd.tensor_tensor(out=result[:], in0=result[:], in1=bias_all[:, bias_cols], op=ALU.add)
+                    nc.gpsimd.tensor_tensor(out=result[:], in0=result[:], in1=bias_long_way[:, cols], op=ALU.add)
+                    late_stores.append((i, w, c, result))
                 else:
                     nc.vector.tensor_tensor(out=result[:], in0=acc[:], in1=bias_all[:, bias_cols], op=ALU.add)
                     store(i, w, c, result)
-                finished.append(result)
-            return finished
 
         def in_range(i):
             return 0 <= i < N_TILES
 
         for s in range(-LEAD_STATS, N_TILES):
+            late_stores = []
             if in_range(s):
-                long_way_results = project(s, 0)
-                project(s, 1)
+                project(s, 0, late_stores)
+                project(s, 1, late_stores)
             if in_range(s + LEAD_QUANTISE):
                 quantise(s + LEAD_QUANTISE)
             if in_range(s):
-                project(s, 2)
-                for c in range(CHUNKS):
-                    store(s, LONG_WAY, c, long_way_results[c])
+                project(s, 2, late_stores)
+            for i, w, c, result in late_stores:
+                store(i, w, c, result)
             if in_range(s + LEAD_TRANSPOSE):
                 transpose_and_scale(s + LEAD_TRANSPOSE)
                 regroup(s + LEAD_TRANSPOSE)
@@ -281,5 +282,7 @@ def tile_swidtblock_pa_kernel(
             if s == -LEAD_STATS:
                 nc.vector.tensor_copy(out=gain_col[:], in_=gain_bf[:].rearrange("p g t -> p (g t)"))
                 nc.vector.tensor_copy(out=beta_col[:], in_=beta_bf[:].rearrange("p g t -> p (g t)"))
+            if s == -LEAD_TRANSPOSE:
+                nc.vector.tensor_copy(out=bias_long_way[:], in_=bias_all[:, LONG_WAY * A : (LONG_WAY + 1) * A])
             if in_range(s + LEAD_NORMALISE):
                 normalise(s + LEAD_NORMALISE)

@@ -96,7 +96,6 @@ def tile_swidtblock_pa_kernel(
         gain_bf = keep.tile([P, PASSES, PACK], BF16)
         beta_bf = keep.tile([P, PASSES, PACK], BF16)
         gain_col = keep.tile([P, PASSES * PACK], F32)
-        beta_col = keep.tile([P, PASSES * PACK], F32)
 
         nc.vector.memset(bias_rows[:].bitcast(I32), 0)
         for w in range(WEIGHTS):
@@ -122,6 +121,8 @@ def tile_swidtblock_pa_kernel(
             )
 
         load_x(0)
+        nc.scalar.dma_start(out=gain_bf[:], in_=ln1_gain.rearrange("(g p t) -> p g t", p=P, t=PACK))
+        nc.scalar.dma_start(out=beta_bf[:], in_=ln1_bias.rearrange("(g p t) -> p g t", p=P, t=PACK))
         nc.gpsimd.memset(minus_half[:], -0.5)
         make_identity(nc, ident[:])
         for w in range(WEIGHTS):
@@ -133,8 +134,6 @@ def tile_swidtblock_pa_kernel(
             )
         load_x(1)
         load_x(2)
-        nc.scalar.dma_start(out=gain_bf[:], in_=ln1_gain.rearrange("(g p t) -> p g t", p=P, t=PACK))
-        nc.scalar.dma_start(out=beta_bf[:], in_=ln1_bias.rearrange("(g p t) -> p g t", p=P, t=PACK))
         for w in range(WEIGHTS):
             load_scales(w)
         load_x(3)
@@ -143,8 +142,10 @@ def tile_swidtblock_pa_kernel(
             in_=x_rows[SINGLE_X_LOADS * P :, :].rearrange("(i p) d -> p i d", p=P),
         )
 
+        spreads = []
         for w in range(WEIGHTS):
             spread = banks.tile([P, A], BF16, tag="bank")
+            spreads.append(spread)
             for c in range(CHUNKS):
                 cols = slice(c * CHUNK, (c + 1) * CHUNK)
                 nc.tensor.matmul(
@@ -154,7 +155,7 @@ def tile_swidtblock_pa_kernel(
                     start=True,
                     stop=True,
                 )
-            nc.scalar.copy(out=bias_all[:, w * A : (w + 1) * A], in_=spread[:])
+        nc.scalar.copy(out=gain_col[:], in_=gain_bf[:].rearrange("p g t -> p (g t)"))
 
         centre = {}
         n_sorted = {}
@@ -208,7 +209,7 @@ def tile_swidtblock_pa_kernel(
                         in_=turned[:, t, :],
                         func=ACT.Identity,
                         scale=gain_col[:, col : col + 1],
-                        bias=beta_col[:, col : col + 1],
+                        bias=beta_bf[:, g, t : t + 1],
                     )
             h_planes[i] = planes
 
@@ -257,7 +258,8 @@ def tile_swidtblock_pa_kernel(
                     nc.gpsimd.tensor_tensor(out=result[:], in0=result[:], in1=bias_long_way[:, cols], op=ALU.add)
                     late_stores.append((i, w, c, result))
                 else:
-                    nc.vector.tensor_tensor(out=result[:], in0=acc[:], in1=bias_all[:, bias_cols], op=ALU.add)
+                    bias = bias_long_way[:, cols] if w == LONG_WAY else bias_all[:, bias_cols]
+                    nc.vector.tensor_tensor(out=result[:], in0=acc[:], in1=bias, op=ALU.add)
                     store(i, w, c, result)
 
         def in_range(i):
@@ -279,10 +281,11 @@ def tile_swidtblock_pa_kernel(
                 regroup(s + LEAD_TRANSPOSE)
             if in_range(s + LEAD_STATS):
                 stats(s + LEAD_STATS)
-            if s == -LEAD_STATS:
-                nc.vector.tensor_copy(out=gain_col[:], in_=gain_bf[:].rearrange("p g t -> p (g t)"))
-                nc.vector.tensor_copy(out=beta_col[:], in_=beta_bf[:].rearrange("p g t -> p (g t)"))
             if s == -LEAD_TRANSPOSE:
-                nc.vector.tensor_copy(out=bias_long_way[:], in_=bias_all[:, LONG_WAY * A : (LONG_WAY + 1) * A])
+                for w in range(WEIGHTS):
+                    if w == LONG_WAY:
+                        nc.vector.tensor_copy(out=bias_long_way[:], in_=spreads[w][:])
+                    else:
+                        nc.vector.tensor_copy(out=bias_all[:, w * A : (w + 1) * A], in_=spreads[w][:])
             if in_range(s + LEAD_NORMALISE):
                 normalise(s + LEAD_NORMALISE)

@@ -92,7 +92,6 @@ def tile_swidtblock_pa_kernel(
         bias_long_way = keep.tile([P, A], F32)
         ones = keep.tile([P, P], BF16)
         ident = keep.tile([P, P], F32)
-        minus_half = keep.tile([P, 1], F32)
         gain_bf = keep.tile([P, PASSES, PACK], BF16)
         beta_bf = keep.tile([P, PASSES, PACK], BF16)
         gain_col = keep.tile([P, PASSES * PACK], F32)
@@ -123,7 +122,6 @@ def tile_swidtblock_pa_kernel(
         load_x(0)
         nc.scalar.dma_start(out=gain_bf[:], in_=ln1_gain.rearrange("(g p t) -> p g t", p=P, t=PACK))
         nc.scalar.dma_start(out=beta_bf[:], in_=ln1_bias.rearrange("(g p t) -> p g t", p=P, t=PACK))
-        nc.gpsimd.memset(minus_half[:], -0.5)
         make_identity(nc, ident[:])
         for w in range(WEIGHTS):
             load_words(w)
@@ -157,6 +155,7 @@ def tile_swidtblock_pa_kernel(
                 )
         nc.scalar.copy(out=gain_col[:], in_=gain_bf[:].rearrange("p g t -> p (g t)"))
 
+        moments = {}
         centre = {}
         n_sorted = {}
         h_planes = {}
@@ -170,19 +169,18 @@ def tile_swidtblock_pa_kernel(
                 nc.vector.bn_stats(out=partial[:, g, :], in_=x_tiles[i][:, g * K_PASS : (g + 1) * K_PASS])
             mean_var = small.tile([P, 2], F32)
             nc.vector.bn_aggr(out=mean_var[:], in_=partial[:].rearrange("p g s -> p (g s)"))
-            shifted = small.tile([P, 2], F32)
-            nc.vector.tensor_scalar(
-                out=shifted[:, 0:1], in0=mean_var[:, 0:1], scalar1=-1.0, scalar2=None, op0=ALU.mult
-            )
-            nc.vector.tensor_scalar(
-                out=shifted[:, 1:2], in0=mean_var[:, 1:2], scalar1=EPS, scalar2=None, op0=ALU.add
-            )
-            centre[i] = shifted
+            moments[i] = mean_var
+
+        def prepare(i):
+            mean_var = moments[i]
+            shifted = small.tile([P, 1], F32)
+            nc.scalar.activation(out=shifted[:], in_=mean_var[:, 0:1], func=ACT.Copy, scale=-1.0)
+            rstd = small.tile([P, 1], F32)
+            nc.scalar.activation(out=rstd[:], in_=mean_var[:, 1:2], func=ACT.Abs_reciprocal_sqrt, bias=EPS, scale=1.0)
+            centre[i] = (shifted, rstd)
 
         def normalise(i):
-            shifted = centre[i]
-            rstd = small.tile([P, 1], F32)
-            nc.gpsimd.tensor_tensor(out=rstd[:], in0=shifted[:, 1:2], in1=minus_half[:], op=ALU.pow)
+            shifted, rstd = centre[i]
             for g in range(PASSES):
                 n_half = work.tile([P, K_PASS], F32, bufs=6)
                 nc.gpsimd.tensor_scalar(
@@ -276,6 +274,8 @@ def tile_swidtblock_pa_kernel(
                 project(s, 2, late_stores)
             for i, w, c, result in late_stores:
                 store(i, w, c, result)
+            if in_range(s + LEAD_NORMALISE):
+                prepare(s + LEAD_NORMALISE)
             if in_range(s + LEAD_TRANSPOSE):
                 transpose_and_scale(s + LEAD_TRANSPOSE)
                 regroup(s + LEAD_TRANSPOSE)

@@ -92,14 +92,15 @@ def tile_swidtblock_pa_kernel(
         bias_long_way = keep.tile([P, A], F32)
         ones = keep.tile([P, P], BF16)
         ident = keep.tile([P, P], F32)
+        one_col = keep.tile([P, 1], F32)
+        table_warmer = keep.tile([P, 1], F32)
         gain_bf = keep.tile([P, PASSES, PACK], BF16)
         beta_bf = keep.tile([P, PASSES, PACK], BF16)
         gain_col = keep.tile([P, PASSES * PACK], F32)
 
-        nc.vector.memset(bias_rows[:].bitcast(I32), 0)
         for w in range(WEIGHTS):
             nc.vector.memset(w_planes[w][:].bitcast(I32), 0)
-        nc.vector.memset(ones[:], 1.0)
+        nc.vector.memset(bias_rows[:].bitcast(I32), 0)
 
         def load_x(i):
             nc.sync.dma_start(out=x_tiles[i], in_=x_rows[i * P : (i + 1) * P, :])
@@ -122,9 +123,12 @@ def tile_swidtblock_pa_kernel(
         load_x(0)
         nc.scalar.dma_start(out=gain_bf[:], in_=ln1_gain.rearrange("(g p t) -> p g t", p=P, t=PACK))
         nc.scalar.dma_start(out=beta_bf[:], in_=ln1_bias.rearrange("(g p t) -> p g t", p=P, t=PACK))
+        nc.gpsimd.memset(one_col[:], 1.0)
+        nc.scalar.activation(out=table_warmer[:], in_=one_col[:], func=ACT.Abs_reciprocal_sqrt)
         make_identity(nc, ident[:])
         for w in range(WEIGHTS):
             load_words(w)
+        nc.gpsimd.memset(ones[:], 1.0)
         for w in range(WEIGHTS):
             nc.scalar.dma_start(
                 out=bias_rows[0:1, w * A : (w + 1) * A],
@@ -141,19 +145,20 @@ def tile_swidtblock_pa_kernel(
         )
 
         spreads = []
-        for w in range(WEIGHTS):
-            spread = banks.tile([P, A], BF16, tag="bank")
-            spreads.append(spread)
-            for c in range(CHUNKS):
-                cols = slice(c * CHUNK, (c + 1) * CHUNK)
-                nc.tensor.matmul(
-                    out=spread[:, cols],
-                    lhsT=ones[:],
-                    rhs=bias_rows[:, w * A + c * CHUNK : w * A + (c + 1) * CHUNK],
-                    start=True,
-                    stop=True,
-                )
-        nc.scalar.copy(out=gain_col[:], in_=gain_bf[:].rearrange("p g t -> p (g t)"))
+
+        def spread_biases():
+            for w in range(WEIGHTS):
+                spread = banks.tile([P, A], BF16, tag="bank")
+                spreads.append(spread)
+                for c in range(CHUNKS):
+                    cols = slice(c * CHUNK, (c + 1) * CHUNK)
+                    nc.tensor.matmul(
+                        out=spread[:, cols],
+                        lhsT=ones[:],
+                        rhs=bias_rows[:, w * A + c * CHUNK : w * A + (c + 1) * CHUNK],
+                        start=True,
+                        stop=True,
+                    )
 
         moments = {}
         centre = {}
@@ -181,9 +186,10 @@ def tile_swidtblock_pa_kernel(
 
         def normalise(i):
             shifted, rstd = centre[i]
+            engine = nc.vector if i == 0 else nc.gpsimd
             for g in range(PASSES):
                 n_half = work.tile([P, K_PASS], F32, bufs=6)
-                nc.gpsimd.tensor_scalar(
+                engine.tensor_scalar(
                     out=n_half[:].rearrange("r (t p) -> r t p", t=PACK),
                     in0=x_tiles[i][:, g * K_PASS : (g + 1) * K_PASS].rearrange("r (p t) -> r t p", t=PACK),
                     scalar1=shifted[:, 0:1],
@@ -276,8 +282,13 @@ def tile_swidtblock_pa_kernel(
                 store(i, w, c, result)
             if in_range(s + LEAD_NORMALISE):
                 prepare(s + LEAD_NORMALISE)
+            if s + LEAD_NORMALISE == 0:
+                normalise(0)
+                nc.scalar.copy(out=gain_col[:], in_=gain_bf[:].rearrange("p g t -> p (g t)"))
             if in_range(s + LEAD_TRANSPOSE):
                 transpose_and_scale(s + LEAD_TRANSPOSE)
+                if s + LEAD_TRANSPOSE == 0:
+                    spread_biases()
                 regroup(s + LEAD_TRANSPOSE)
             if in_range(s + LEAD_STATS):
                 stats(s + LEAD_STATS)
@@ -287,5 +298,5 @@ def tile_swidtblock_pa_kernel(
                         nc.vector.tensor_copy(out=bias_long_way[:], in_=spreads[w][:])
                     else:
                         nc.vector.tensor_copy(out=bias_all[:, w * A : (w + 1) * A], in_=spreads[w][:])
-            if in_range(s + LEAD_NORMALISE):
+            if in_range(s + LEAD_NORMALISE) and s + LEAD_NORMALISE > 0:
                 normalise(s + LEAD_NORMALISE)

@@ -200,7 +200,7 @@ def tile_swidtblock_pa_kernel(
                 n_sorted[(i, g)] = n_half
 
         def transpose_and_scale(i):
-            planes = work.tile([P, PASSES, PACK, P], BF16)
+            planes = work.tile([P, PASSES, 2, P, 2], BF16)
             for g in range(PASSES):
                 n_half = n_sorted[(i, g)]
                 turned = flipped.tile([P, PACK, P], F32)
@@ -209,7 +209,7 @@ def tile_swidtblock_pa_kernel(
                 for t in range(PACK):
                     col = g * PACK + t
                     nc.scalar.activation(
-                        out=planes[:, g, t, :],
+                        out=planes[:, g, t // 2, :, t % 2],
                         in_=turned[:, t, :],
                         func=ACT.Identity,
                         scale=gain_col[:, col : col + 1],
@@ -220,10 +220,12 @@ def tile_swidtblock_pa_kernel(
         def regroup(i):
             planes = h_planes[i]
             grouped = work.tile([P, PASSES * P * PACK], BF16, align_bytes=64)
-            nc.scalar.copy(
-                out=grouped[:].rearrange("p (g r t) -> p g r t", g=PASSES, t=PACK),
-                in_=planes[:].rearrange("p g t r -> p g r t"),
-            )
+            for g in range(PASSES):
+                half = slice(g * P * PACK, (g + 1) * P * PACK)
+                nc.scalar.copy(
+                    out=grouped[:, half].bitcast(F32).rearrange("p (r u) -> p r u", u=2),
+                    in_=planes[:, g, :, :, :].rearrange("p u r e -> p (u r e)").bitcast(F32).rearrange("p (u r) -> p r u", u=2),
+                )
             h_grouped[i] = grouped
 
         def quantise(i):

@@ -68,7 +68,7 @@ def tile_swidtblock_pa_kernel(
         keep = ctx.enter_context(tc.tile_pool(name="keep", bufs=1))
         small = ctx.enter_context(tc.tile_pool(name="small", bufs=6))
         work = ctx.enter_context(tc.tile_pool(name="work", bufs=3))
-        results = ctx.enter_context(tc.tile_pool(name="results", bufs=16))
+        results = ctx.enter_context(tc.tile_pool(name="results", bufs=10))
         banks = ctx.enter_context(tc.psum_pool(name="banks", bufs=6))
         flipped = ctx.enter_context(tc.psum_pool(name="flipped", bufs=2))
 
@@ -160,6 +160,7 @@ def tile_swidtblock_pa_kernel(
                         stop=True,
                     )
 
+        partials = {}
         moments = {}
         centre = {}
         n_sorted = {}
@@ -168,10 +169,14 @@ def tile_swidtblock_pa_kernel(
         h_codes = {}
         h_scales = {}
 
-        def stats(i):
+        def sums(i):
             partial = small.tile([P, PASSES, 6], F32)
+            partials[i] = partial
             for g in range(PASSES):
                 nc.vector.bn_stats(out=partial[:, g, :], in_=x_tiles[i][:, g * K_PASS : (g + 1) * K_PASS])
+
+        def aggregate(i):
+            partial = partials[i]
             mean_var = small.tile([P, 2], F32)
             nc.vector.bn_aggr(out=mean_var[:], in_=partial[:].rearrange("p g s -> p (g s)"))
             moments[i] = mean_var
@@ -199,9 +204,11 @@ def tile_swidtblock_pa_kernel(
                 )
                 n_sorted[(i, g)] = n_half
 
-        def transpose_and_scale(i):
+        def transpose_and_scale(i, between=None):
             planes = work.tile([P, PASSES, 2, P, 2], BF16)
             for g in range(PASSES):
+                if g == 1 and between is not None:
+                    between()
                 n_half = n_sorted[(i, g)]
                 turned = flipped.tile([P, PACK, P], F32)
                 for t in range(PACK):
@@ -236,17 +243,18 @@ def tile_swidtblock_pa_kernel(
             h_codes[i] = codes
             h_scales[i] = scales
 
-        def store(i, w, c, result):
-            nc.sync.dma_start(out=outs[w][i * P : (i + 1) * P, c * CHUNK : (c + 1) * CHUNK], in_=result[:])
+        def store(i, w, result):
+            nc.sync.dma_start(out=outs[w][i * P : (i + 1) * P, :], in_=result[:])
 
         def vector_has_stats(i):
             return i + LEAD_STATS < N_TILES
 
         def project(i, w, late_stores):
+            result = results.tile([P, A], F32)
+            long_way = w == LONG_WAY and vector_has_stats(i)
             for c in range(CHUNKS):
                 cols = slice(c * CHUNK, (c + 1) * CHUNK)
                 bias_cols = slice(w * A + c * CHUNK, w * A + (c + 1) * CHUNK)
-                result = results.tile([P, CHUNK], F32)
                 acc = banks.tile([P, CHUNK], F32, tag="bank")
                 for g in range(PASSES):
                     tokens = slice(g * P, (g + 1) * P)
@@ -259,46 +267,65 @@ def tile_swidtblock_pa_kernel(
                         start=(g == 0),
                         stop=(g == PASSES - 1),
                     )
-                if w == LONG_WAY and vector_has_stats(i):
-                    nc.scalar.copy(out=result[:], in_=acc[:])
-                    nc.gpsimd.tensor_tensor(out=result[:], in0=result[:], in1=bias_long_way[:, cols], op=ALU.add)
-                    late_stores.append((i, w, c, result))
+                if long_way:
+                    nc.scalar.copy(out=result[:, cols], in_=acc[:])
+                    nc.gpsimd.tensor_tensor(
+                        out=result[:, cols], in0=result[:, cols], in1=bias_long_way[:, cols], op=ALU.add
+                    )
                 else:
                     bias = bias_long_way[:, cols] if w == LONG_WAY else bias_all[:, bias_cols]
-                    nc.vector.tensor_tensor(out=result[:], in0=acc[:], in1=bias, op=ALU.add)
-                    store(i, w, c, result)
+                    nc.vector.tensor_tensor(out=result[:, cols], in0=acc[:], in1=bias, op=ALU.add)
+            if long_way:
+                late_stores.append((i, w, result))
+            else:
+                store(i, w, result)
 
         def in_range(i):
             return 0 <= i < N_TILES
 
-        for s in range(-LEAD_STATS, N_TILES):
+        sums(0)
+        aggregate(0)
+        prepare(0)
+        normalise(0)
+        nc.scalar.copy(out=gain_col[:], in_=gain_bf[:].rearrange("p g t -> p (g t)"))
+        sums(1)
+        aggregate(1)
+        transpose_and_scale(0, lambda: prepare(1))
+        spread_biases()
+        regroup(0)
+        sums(2)
+        aggregate(2)
+        for w in range(WEIGHTS):
+            if w == LONG_WAY:
+                nc.vector.tensor_copy(out=bias_long_way[:], in_=spreads[w][:])
+            else:
+                nc.vector.tensor_copy(out=bias_all[:, w * A : (w + 1) * A], in_=spreads[w][:])
+        normalise(1)
+        quantise(0)
+        prepare(2)
+        transpose_and_scale(1)
+        regroup(1)
+        sums(3)
+        aggregate(3)
+        normalise(2)
+
+        for s in range(N_TILES):
             late_stores = []
-            if in_range(s):
-                project(s, 0, late_stores)
-                project(s, 1, late_stores)
+            project(s, 0, late_stores)
             if in_range(s + LEAD_QUANTISE):
                 quantise(s + LEAD_QUANTISE)
-            if in_range(s):
-                project(s, 2, late_stores)
-            for i, w, c, result in late_stores:
-                store(i, w, c, result)
+            project(s, 1, late_stores)
+            for i, w, result in late_stores:
+                store(i, w, result)
             if in_range(s + LEAD_NORMALISE):
                 prepare(s + LEAD_NORMALISE)
-            if s + LEAD_NORMALISE == 0:
-                normalise(0)
-                nc.scalar.copy(out=gain_col[:], in_=gain_bf[:].rearrange("p g t -> p (g t)"))
             if in_range(s + LEAD_TRANSPOSE):
                 transpose_and_scale(s + LEAD_TRANSPOSE)
-                if s + LEAD_TRANSPOSE == 0:
-                    spread_biases()
                 regroup(s + LEAD_TRANSPOSE)
-            if in_range(s + LEAD_STATS):
-                stats(s + LEAD_STATS)
-            if s == -LEAD_TRANSPOSE:
-                for w in range(WEIGHTS):
-                    if w == LONG_WAY:
-                        nc.vector.tensor_copy(out=bias_long_way[:], in_=spreads[w][:])
-                    else:
-                        nc.vector.tensor_copy(out=bias_all[:, w * A : (w + 1) * A], in_=spreads[w][:])
-            if in_range(s + LEAD_NORMALISE) and s + LEAD_NORMALISE > 0:
+            if in_range(s + LEAD_NORMALISE):
                 normalise(s + LEAD_NORMALISE)
+            if in_range(s + LEAD_STATS):
+                sums(s + LEAD_STATS)
+            project(s, 2, late_stores)
+            if in_range(s + LEAD_STATS):
+                aggregate(s + LEAD_STATS)

@@ -32,7 +32,7 @@ LEAD_NORMALISE = 3
 LEAD_TRANSPOSE = 2
 LEAD_QUANTISE = 1
 
-SINGLE_X_LOADS = 4
+X_LOADS = (1, 1, 2, 4)
 LONG_WAY = 0
 
 FLOPS = 2 * TOKENS * D * WEIGHTS * A
@@ -73,12 +73,12 @@ def tile_swidtblock_pa_kernel(
         flipped = ctx.enter_context(tc.psum_pool(name="flipped", bufs=2))
 
         x_tiles = []
-        for i in range(SINGLE_X_LOADS):
-            x_tile = keep.tile([P, D], BF16, name="x%d" % i)
-            x_tiles.append(x_tile[:])
-        x_rest = keep.tile([P, N_TILES - SINGLE_X_LOADS, D], BF16)
-        for i in range(SINGLE_X_LOADS, N_TILES):
-            x_tiles.append(x_rest[:, i - SINGLE_X_LOADS, :])
+        x_groups = []
+        for n, count in enumerate(X_LOADS):
+            x_group = keep.tile([P, count, D], BF16, name="x%d" % n)
+            x_groups.append((len(x_tiles), count, x_group))
+            for j in range(count):
+                x_tiles.append(x_group[:, j, :])
         w_words = []
         for w in range(WEIGHTS):
             w_tile = keep.tile([P, PASSES, A], U32, name="w_words%d" % w, align_bytes=64)
@@ -99,11 +99,16 @@ def tile_swidtblock_pa_kernel(
         gain_col = keep.tile([P, PASSES * PACK], F32)
 
         for w in range(WEIGHTS):
+            nc.vector.memset(bias_rows[:, w * A : (w + 1) * A].bitcast(I32), 0)
+        for w in range(WEIGHTS):
             nc.vector.memset(w_planes[w][:].bitcast(I32), 0)
-        nc.vector.memset(bias_rows[:].bitcast(I32), 0)
 
         def load_x(i):
-            nc.sync.dma_start(out=x_tiles[i], in_=x_rows[i * P : (i + 1) * P, :])
+            first, count, x_group = x_groups[i]
+            nc.sync.dma_start(
+                out=x_group[:],
+                in_=x_rows[first * P : (first + count) * P, :].rearrange("(i p) d -> p i d", p=P),
+            )
 
         def load_scales(w):
             for quadrant in range(QUADRANTS):
@@ -121,6 +126,8 @@ def tile_swidtblock_pa_kernel(
             )
 
         load_x(0)
+        load_x(1)
+        load_x(2)
         nc.scalar.dma_start(out=gain_bf[:], in_=ln1_gain.rearrange("(g p t) -> p g t", p=P, t=PACK))
         nc.scalar.dma_start(out=beta_bf[:], in_=ln1_bias.rearrange("(g p t) -> p g t", p=P, t=PACK))
         nc.gpsimd.memset(one_col[:], 1.0)
@@ -134,15 +141,9 @@ def tile_swidtblock_pa_kernel(
                 out=bias_rows[0:1, w * A : (w + 1) * A],
                 in_=biases_in[w].rearrange("(o n) -> o n", o=1),
             )
-        load_x(1)
-        load_x(2)
         for w in range(WEIGHTS):
             load_scales(w)
         load_x(3)
-        nc.sync.dma_start(
-            out=x_rest[:],
-            in_=x_rows[SINGLE_X_LOADS * P :, :].rearrange("(i p) d -> p i d", p=P),
-        )
 
         spreads = []
 
@@ -243,8 +244,8 @@ def tile_swidtblock_pa_kernel(
             h_codes[i] = codes
             h_scales[i] = scales
 
-        def store(i, w, result):
-            nc.sync.dma_start(out=outs[w][i * P : (i + 1) * P, :], in_=result[:])
+        def store(i, w, result, cols=slice(0, A)):
+            nc.sync.dma_start(out=outs[w][i * P : (i + 1) * P, cols], in_=result[:, cols])
 
         def vector_has_stats(i):
             return i + LEAD_STATS < N_TILES
@@ -252,6 +253,7 @@ def tile_swidtblock_pa_kernel(
         def project(i, w, late_stores):
             result = results.tile([P, A], F32)
             long_way = w == LONG_WAY and vector_has_stats(i)
+            last = i == N_TILES - 1 and w == WEIGHTS - 1
             for c in range(CHUNKS):
                 cols = slice(c * CHUNK, (c + 1) * CHUNK)
                 bias_cols = slice(w * A + c * CHUNK, w * A + (c + 1) * CHUNK)
@@ -275,9 +277,11 @@ def tile_swidtblock_pa_kernel(
                 else:
                     bias = bias_long_way[:, cols] if w == LONG_WAY else bias_all[:, bias_cols]
                     nc.vector.tensor_tensor(out=result[:, cols], in0=acc[:], in1=bias, op=ALU.add)
+                    if last:
+                        store(i, w, result, cols)
             if long_way:
                 late_stores.append((i, w, result))
-            else:
+            elif not last:
                 store(i, w, result)
 
         def in_range(i):
@@ -295,19 +299,19 @@ def tile_swidtblock_pa_kernel(
         regroup(0)
         sums(2)
         aggregate(2)
+        prepare(2)
+        normalise(1)
+        normalise(2)
+        quantise(0)
         for w in range(WEIGHTS):
             if w == LONG_WAY:
                 nc.vector.tensor_copy(out=bias_long_way[:], in_=spreads[w][:])
             else:
                 nc.vector.tensor_copy(out=bias_all[:, w * A : (w + 1) * A], in_=spreads[w][:])
-        normalise(1)
-        quantise(0)
-        prepare(2)
         transpose_and_scale(1)
         regroup(1)
         sums(3)
         aggregate(3)
-        normalise(2)
 
         for s in range(N_TILES):
             late_stores = []

from contextlib import ExitStack

import concourse.mybir as mybir
from concourse.masks import make_identity

F32 = mybir.dt.float32
BF16 = mybir.dt.bfloat16
I32 = mybir.dt.int32
U32 = mybir.dt.uint32
U8 = mybir.dt.uint8
FP8X4 = mybir.dt.float8_e4m3fn_x4
ALU = mybir.AluOpType
ACT = mybir.ActivationFunctionType

P = 128
PACK = 4
K_PASS = P * PACK
TOKENS = 4 * 256
D = 1024
A = 1024
EPS = 1e-6
N_TILES = TOKENS // P
PASSES = D // K_PASS
CHUNK = 512
CHUNKS = A // CHUNK
WEIGHTS = 3
QUADRANTS = 4
SCALE_ROWS = 4

LEAD_STATS = 4
LEAD_NORMALISE = 3
LEAD_TRANSPOSE = 2
LEAD_QUANTISE = 1

X_LOADS = (1, 1, 2, 4)
LONG_WAY = 0

FLOPS = 2 * TOKENS * D * WEIGHTS * A


def tile_swidtblock_pa_kernel(
    tc,
    x,
    ln1_gain,
    ln1_bias,
    wq_words,
    wq_scales,
    bq,
    wk_words,
    wk_scales,
    bk,
    wv_words,
    wv_scales,
    bv,
    out_0,
    out_1,
    out_2,
):
    nc = tc.nc
    x_rows = x.rearrange("b t d -> (b t) d")
    words_in = [wq_words, wk_words, wv_words]
    scales_in = [wq_scales, wk_scales, wv_scales]
    biases_in = [bq, bk, bv]
    outs = [o.rearrange("b t h d -> (b t) (h d)") for o in (out_0, out_1, out_2)]

    with ExitStack() as ctx:
        ctx.enter_context(tc.manual_schedule())
        keep = ctx.enter_context(tc.tile_pool(name="keep", bufs=1))
        small = ctx.enter_context(tc.tile_pool(name="small", bufs=6))
        work = ctx.enter_context(tc.tile_pool(name="work", bufs=3))
        results = ctx.enter_context(tc.tile_pool(name="results", bufs=10))
        banks = ctx.enter_context(tc.psum_pool(name="banks", bufs=6))
        flipped = ctx.enter_context(tc.psum_pool(name="flipped", bufs=2))

        x_tiles = []
        x_groups = []
        for n, count in enumerate(X_LOADS):
            x_group = keep.tile([P, count, D], BF16, name="x%d" % n)
            x_groups.append((len(x_tiles), count, x_group))
            for j in range(count):
                x_tiles.append(x_group[:, j, :])
        w_words = []
        for w in range(WEIGHTS):
            w_tile = keep.tile([P, PASSES, A], U32, name="w_words%d" % w, align_bytes=64)
            w_words.append(w_tile)
        w_planes = []
        for w in range(WEIGHTS):
            plane_tile = keep.tile([P, A], U8, name="w_planes%d" % w, align_bytes=64)
            w_planes.append(plane_tile)
        bias_rows = keep.tile([P, WEIGHTS * A], BF16)
        bias_all = keep.tile([P, WEIGHTS * A], BF16)
        bias_long_way = keep.tile([P, A], F32)
        ones = keep.tile([P, P], BF16)
        ident = keep.tile([P, P], F32)
        one_col = keep.tile([P, 1], F32)
        table_warmer = keep.tile([P, 1], F32)
        gain_bf = keep.tile([P, PASSES, PACK], BF16)
        beta_bf = keep.tile([P, PASSES, PACK], BF16)
        gain_col = keep.tile([P, PASSES * PACK], F32)

        for w in range(WEIGHTS):
            nc.vector.memset(bias_rows[:, w * A : (w + 1) * A].bitcast(I32), 0)
        for w in range(WEIGHTS):
            nc.vector.memset(w_planes[w][:].bitcast(I32), 0)

        def load_x(i):
            first, count, x_group = x_groups[i]
            nc.sync.dma_start(
                out=x_group[:],
                in_=x_rows[first * P : (first + count) * P, :].rearrange("(i p) d -> p i d", p=P),
            )

        def load_scales(w):
            for quadrant in range(QUADRANTS):
                first = 32 * quadrant
                rows = slice(SCALE_ROWS * quadrant, SCALE_ROWS * (quadrant + 1))
                nc.sync.dma_start(
                    out=w_planes[w][first : first + PASSES * SCALE_ROWS, :].bitcast(I32),
                    in_=scales_in[w][:, rows, :].bitcast(I32),
                )

        def load_words(w):
            nc.gpsimd.dma_start(
                out=w_words[w][:].bitcast(F32),
                in_=words_in[w].rearrange("g p n t -> p g (n t)").bitcast(F32),
            )

        load_x(0)
        load_x(1)
        load_x(2)
        nc.scalar.dma_start(out=gain_bf[:], in_=ln1_gain.rearrange("(g p t) -> p g t", p=P, t=PACK))
        nc.scalar.dma_start(out=beta_bf[:], in_=ln1_bias.rearrange("(g p t) -> p g t", p=P, t=PACK))
        nc.gpsimd.memset(one_col[:], 1.0)
        nc.scalar.activation(out=table_warmer[:], in_=one_col[:], func=ACT.Abs_reciprocal_sqrt)
        make_identity(nc, ident[:])
        for w in range(WEIGHTS):
            load_words(w)
        nc.gpsimd.memset(ones[:], 1.0)
        for w in range(WEIGHTS):
            nc.scalar.dma_start(
                out=bias_rows[0:1, w * A : (w + 1) * A],
                in_=biases_in[w].rearrange("(o n) -> o n", o=1),
            )
        for w in range(WEIGHTS):
            load_scales(w)
        load_x(3)

        spreads = []

        def spread_biases():
            for w in range(WEIGHTS):
                spread = banks.tile([P, A], BF16, tag="bank")
                spreads.append(spread)
                for c in range(CHUNKS):
                    cols = slice(c * CHUNK, (c + 1) * CHUNK)
                    nc.tensor.matmul(
                        out=spread[:, cols],
                        lhsT=ones[:],
                        rhs=bias_rows[:, w * A + c * CHUNK : w * A + (c + 1) * CHUNK],
                        start=True,
                        stop=True,
                    )

        partials = {}
        moments = {}
        centre = {}
        n_sorted = {}
        h_planes = {}
        h_grouped = {}
        h_codes = {}
        h_scales = {}

        def sums(i):
            partial = small.tile([P, PASSES, 6], F32)
            partials[i] = partial
            for g in range(PASSES):
                nc.vector.bn_stats(out=partial[:, g, :], in_=x_tiles[i][:, g * K_PASS : (g + 1) * K_PASS])

        def aggregate(i):
            partial = partials[i]
            mean_var = small.tile([P, 2], F32)
            nc.vector.bn_aggr(out=mean_var[:], in_=partial[:].rearrange("p g s -> p (g s)"))
            moments[i] = mean_var

        def prepare(i):
            mean_var = moments[i]
            shifted = small.tile([P, 1], F32)
            nc.scalar.activation(out=shifted[:], in_=mean_var[:, 0:1], func=ACT.Copy, scale=-1.0)
            rstd = small.tile([P, 1], F32)
            nc.scalar.activation(out=rstd[:], in_=mean_var[:, 1:2], func=ACT.Abs_reciprocal_sqrt, bias=EPS, scale=1.0)
            centre[i] = (shifted, rstd)

        def normalise(i):
            shifted, rstd = centre[i]
            engine = nc.vector if i == 0 else nc.gpsimd
            for g in range(PASSES):
                n_half = work.tile([P, K_PASS], F32, bufs=6)
                engine.tensor_scalar(
                    out=n_half[:].rearrange("r (t p) -> r t p", t=PACK),
                    in0=x_tiles[i][:, g * K_PASS : (g + 1) * K_PASS].rearrange("r (p t) -> r t p", t=PACK),
                    scalar1=shifted[:, 0:1],
                    scalar2=rstd[:, 0:1],
                    op0=ALU.add,
                    op1=ALU.mult,
                )
                n_sorted[(i, g)] = n_half

        def transpose_and_scale(i, between=None):
            planes = work.tile([P, PASSES, 2, P, 2], BF16)
            for g in range(PASSES):
                if g == 1 and between is not None:
                    between()
                n_half = n_sorted[(i, g)]
                turned = flipped.tile([P, PACK, P], F32)
                for t in range(PACK):
                    nc.tensor.transpose(turned[:, t, :], n_half[:, t * P : (t + 1) * P], ident[:])
                for t in range(PACK):
                    col = g * PACK + t
                    nc.scalar.activation(
                        out=planes[:, g, t // 2, :, t % 2],
                        in_=turned[:, t, :],
                        func=ACT.Identity,
                        scale=gain_col[:, col : col + 1],
                        bias=beta_bf[:, g, t : t + 1],
                    )
            h_planes[i] = planes

        def regroup(i):
            planes = h_planes[i]
            grouped = work.tile([P, PASSES * P * PACK], BF16, align_bytes=64)
            for g in range(PASSES):
                half = slice(g * P * PACK, (g + 1) * P * PACK)
                nc.scalar.copy(
                    out=grouped[:, half].bitcast(F32).rearrange("p (r u) -> p r u", u=2),
                    in_=planes[:, g, :, :, :].rearrange("p u r e -> p (u r e)").bitcast(F32).rearrange("p (u r) -> p r u", u=2),
                )
            h_grouped[i] = grouped

        def quantise(i):
            grouped = h_grouped[i]
            codes = work.tile([P, PASSES * P], U32, align_bytes=64)
            scales = work.tile([P, PASSES * P], U8, align_bytes=64)
            nc.vector.quantize_mx(out=codes[:].bitcast(FP8X4), scales=scales[:], in_=grouped[:])
            h_codes[i] = codes
            h_scales[i] = scales

        def store(i, w, result, cols=slice(0, A)):
            nc.sync.dma_start(out=outs[w][i * P : (i + 1) * P, cols], in_=result[:, cols])

        def vector_has_stats(i):
            return i + LEAD_STATS < N_TILES

        def project(i, w, late_stores):
            result = results.tile([P, A], F32)
            long_way = w == LONG_WAY and vector_has_stats(i)
            last = i == N_TILES - 1 and w == WEIGHTS - 1
            for c in range(CHUNKS):
                cols = slice(c * CHUNK, (c + 1) * CHUNK)
                bias_cols = slice(w * A + c * CHUNK, w * A + (c + 1) * CHUNK)
                acc = banks.tile([P, CHUNK], F32, tag="bank")
                for g in range(PASSES):
                    tokens = slice(g * P, (g + 1) * P)
                    nc.tensor.matmul_mx(
                        out=acc[:],
                        lhsT=h_codes[i][:, tokens].bitcast(FP8X4),
                        lhsT_scale=h_scales[i][:, tokens],
                        rhs=w_words[w][:, g, cols].bitcast(FP8X4),
                        rhs_scale=w_planes[w][SCALE_ROWS * g : P, cols],
                        start=(g == 0),
                        stop=(g == PASSES - 1),
                    )
                if long_way:
                    nc.scalar.copy(out=result[:, cols], in_=acc[:])
                    nc.gpsimd.tensor_tensor(
                        out=result[:, cols], in0=result[:, cols], in1=bias_long_way[:, cols], op=ALU.add
                    )
                else:
                    bias = bias_long_way[:, cols] if w == LONG_WAY else bias_all[:, bias_cols]
                    nc.vector.tensor_tensor(out=result[:, cols], in0=acc[:], in1=bias, op=ALU.add)
                    if last:
                        store(i, w, result, cols)
            if long_way:
                late_stores.append((i, w, result))
            elif not last:
                store(i, w, result)

        def in_range(i):
            return 0 <= i < N_TILES

        sums(0)
        aggregate(0)
        prepare(0)
        normalise(0)
        nc.scalar.copy(out=gain_col[:], in_=gain_bf[:].rearrange("p g t -> p (g t)"))
        sums(1)
        aggregate(1)
        transpose_and_scale(0, lambda: prepare(1))
        spread_biases()
        regroup(0)
        sums(2)
        aggregate(2)
        prepare(2)
        normalise(1)
        normalise(2)
        quantise(0)
        for w in range(WEIGHTS):
            if w == LONG_WAY:
                nc.vector.tensor_copy(out=bias_long_way[:], in_=spreads[w][:])
            else:
                nc.vector.tensor_copy(out=bias_all[:, w * A : (w + 1) * A], in_=spreads[w][:])
        transpose_and_scale(1)
        regroup(1)
        sums(3)
        aggregate(3)

        for s in range(N_TILES):
            late_stores = []
            project(s, 0, late_stores)
            if in_range(s + LEAD_QUANTISE):
                quantise(s + LEAD_QUANTISE)
            project(s, 1, late_stores)
            for i, w, result in late_stores:
                store(i, w, result)
            if in_range(s + LEAD_NORMALISE):
                prepare(s + LEAD_NORMALISE)
            if in_range(s + LEAD_TRANSPOSE):
                transpose_and_scale(s + LEAD_TRANSPOSE)
                regroup(s + LEAD_TRANSPOSE)
            if in_range(s + LEAD_NORMALISE):
                normalise(s + LEAD_NORMALISE)
            if in_range(s + LEAD_STATS):
                sums(s + LEAD_STATS)
            project(s, 2, late_stores)
            if in_range(s + LEAD_STATS):
                aggregate(s + LEAD_STATS)
